import numpy as np
import ml_dtypes


def mxq(x, axis, fmt="e4m3"):
    dtype, down = {"e4m3": (ml_dtypes.float8_e4m3fn, 7), "e5m2": (ml_dtypes.float8_e5m2, 14)}[fmt]
    v = np.moveaxis(np.asarray(x, np.float32).astype(ml_dtypes.bfloat16).astype(np.float64), axis, -1)
    blocks = v.reshape(v.shape[:-1] + (-1, 32))
    amax = np.abs(blocks).max(-1, keepdims=True)
    byte = np.maximum(np.where(amax > 0, np.frexp(amax)[1] - 1 + 127, 0) - down, 1)
    scale = np.exp2(byte - 127.0)
    codes = (blocks / scale).astype(np.float32).astype(dtype).astype(np.float64)
    return np.moveaxis((codes * scale).reshape(v.shape), -1, axis)


WIDE = False


def mx_kscale(k):
    if not WIDE:
        return np.ones(k)
    levels = np.array([10, -10, 5, -5, 0])
    a = np.random.permutation(np.resize(levels, k // 512 * 4)).reshape(k // 512, 4)
    idx = np.arange(k)
    return np.exp2(a[idx // 512, idx % 128 // 32])


BF16 = ml_dtypes.bfloat16


def bf(x):
    return np.asarray(x, np.float32).astype(BF16)


def f64(x):
    return np.asarray(x).astype(np.float64)


E2M1 = np.array([0.0, 0.5, 1.0, 1.5, 2.0, 3.0, 4.0, 6.0, -0.0, -0.5, -1.0, -1.5, -2.0, -3.0, -4.0, -6.0])


def pack_weight(w, fmt):
    k, n = w.shape
    w = f64(bf(w)).reshape(k // 32, 32, n)
    amax = np.abs(w).max(1)
    if fmt == "e4m3":
        byte = np.frexp(amax)[1] - 1 + 127 - 7
    else:
        mant, ex = np.frexp(amax / 6.0)
        byte = np.where(mant > 0.5, ex, ex - 1) + 127
    byte = np.clip(np.where(amax > 0, byte, 1), 1, 254)
    scaled = (w * np.exp2(127.0 - byte)[:, None, :]).reshape(k, n).astype(np.float32)
    by_word = np.ascontiguousarray(scaled.reshape(k // 512, 128, 4, n).transpose(0, 1, 3, 2))
    if fmt == "e4m3":
        words = by_word.astype(ml_dtypes.float8_e4m3fn).view(np.uint8)
    else:
        c = by_word.astype(ml_dtypes.float4_e2m1fn).view(np.uint8) & 0xF
        words = c[..., 0::2] | (c[..., 1::2] << 4)
    return np.ascontiguousarray(words), np.ascontiguousarray(byte.astype(np.uint8).reshape(k // 512, 16, n))


def unpack_weight(words, scales, fmt):
    g, p, n, _ = words.shape
    if fmt == "e4m3":
        vals = np.ascontiguousarray(words).view(ml_dtypes.float8_e4m3fn).astype(np.float64)
    else:
        nib = np.empty((g, p, n, 4), np.uint8)
        nib[..., 0::2] = words & 0xF
        nib[..., 1::2] = words >> 4
        vals = E2M1[nib]
    vals = vals * np.repeat(np.exp2(scales.astype(np.float64) - 127.0), 8, axis=1)[..., None]
    return vals.transpose(0, 1, 3, 2).reshape(g * 512, n)

def pack4(w):
    words, scales = pack_weight(w, "e2m1")
    return words.reshape(words.shape[0], 128, -1), scales


def unpack4(words, scales):
    return unpack_weight(words.reshape(words.shape[0], 128, -1, 2), scales, "e2m1")


B, T, C, H, W = 1, 1536, 1024, 8, 512
D = C // H
HALF = D // 2
ROPE_BASE = 10000.0


def rotate_half(u):
    return np.concatenate([-u[..., HALF:], u[..., :HALF]], axis=-1)


def setup_inputs():
    s = mx_kscale(C)
    start = np.random.randint(0, T)
    inv_freq = 1.0 / (ROPE_BASE ** (np.arange(0, D, 2) / D))
    freqs = np.outer(start + np.arange(T), inv_freq)
    emb = np.concatenate([freqs, freqs], axis=-1)
    x = bf(np.random.standard_normal((B, T, C)) * s)
    words, scales = pack4(np.random.standard_normal((C, 3 * C)) * 1.25 / np.sqrt(C) / s[:, None])
    return {"x": x,
            "freqs_cos": bf(np.cos(emb)),
            "freqs_sin": bf(np.sin(emb)),
            "w_attn_words": words,
            "w_attn_scales": scales}


def reference(x, freqs_cos, freqs_sin, w_attn_words, w_attn_scales):
    qkv = mxq(f64(x), 2, "e4m3") @ unpack4(w_attn_words, w_attn_scales)
    q, k, v = np.split(qkv, 3, axis=-1)
    q = q.reshape(B, T, H, D).transpose(0, 2, 1, 3)
    k = k.reshape(B, T, H, D).transpose(0, 2, 1, 3)
    v = v.reshape(B, T, H, D).transpose(0, 2, 1, 3)
    cos = f64(freqs_cos)[None, None, :, :]
    sin = f64(freqs_sin)[None, None, :, :]
    q_rot = q * cos + rotate_half(q) * sin
    k_rot = k * cos + rotate_half(k) * sin
    return q_rot, k_rot, v

@@ -1,0 +1,180 @@
+from contextlib import ExitStack
+
+import concourse.mybir as mybir
+from concourse.masks import make_identity
+
+F32 = mybir.dt.float32
+BF16 = mybir.dt.bfloat16
+I32 = mybir.dt.int32
+U32 = mybir.dt.uint32
+U8 = mybir.dt.uint8
+FP8X4 = mybir.dt.float8_e4m3fn_x4
+FP4X4 = mybir.dt.float4_e2m1fn_x4
+ALU = mybir.AluOpType
+
+P = 128
+T = 1536
+C = 1024
+D = 128
+HALF = D // 2
+K_PASS = 4 * P
+PASSES = C // K_PASS
+WORDS = K_PASS // 2
+TILES = T // P
+GROUP = 4
+GROUPS = TILES // GROUP
+BLOCK_HEADS = 4
+BLOCK = BLOCK_HEADS * D
+BLOCKS = 3 * C // BLOCK
+
+FLOPS = 2 * T * C * 3 * C
+
+
+def tile_swaattention_pa_kernel(
+    tc, x, freqs_cos, freqs_sin, w_attn_words, w_attn_scales, out_0, out_1, out_2
+):
+    nc = tc.nc
+    outs = [out_0, out_1, out_2]
+
+    x_rows = x[0].rearrange("(p j) c -> p j c", j=TILES)
+    cos_rows = freqs_cos.rearrange("(p j) d -> p j d", j=TILES)
+    sin_rows = freqs_sin.rearrange("(p j) d -> p j d", j=TILES)
+    words_dram = w_attn_words.bitcast(I32).rearrange("g p n -> p g n")
+    scales_dram = w_attn_scales.bitcast(I32).rearrange("g q n -> q g n")
+
+    with ExitStack() as ctx:
+        keep = ctx.enter_context(tc.tile_pool(name="keep", bufs=1))
+        stage = ctx.enter_context(tc.tile_pool(name="stage", bufs=3))
+        rotated = ctx.enter_context(tc.tile_pool(name="rotated", bufs=4))
+        copied = ctx.enter_context(tc.tile_pool(name="copied", bufs=3))
+        psum_x = ctx.enter_context(tc.psum_pool(name="psum_x", bufs=2))
+        psum_qk = ctx.enter_context(tc.psum_pool(name="psum_qk", bufs=4))
+        psum_v = ctx.enter_context(tc.psum_pool(name="psum_v", bufs=2))
+
+        x_sb = keep.tile([P, TILES, C], BF16)
+        w_words = keep.tile([P, PASSES, 2 * 3 * C], U8, align_bytes=64)
+        w_planes = keep.tile([P, PASSES, 3 * C], U8, align_bytes=64)
+        tables = keep.tile([P, 2, TILES, D], BF16)
+        sin_sb = keep.tile([P, TILES, D], BF16)
+        ident = keep.tile([P, P], F32)
+        x_codes = keep.tile([P, TILES, PASSES * P], U32, align_bytes=64)
+        x_planes = keep.tile([P, TILES, PASSES * P], U8, align_bytes=64)
+
+        nc.vector.memset(w_planes[:].bitcast(I32), 0)
+        make_identity(nc, ident[:])
+
+        def load_x(first, count):
+            nc.sync.dma_start(
+                out=x_sb[:, first : first + count, :], in_=x_rows[:, first : first + count, :]
+            )
+
+        def load_w_block(c):
+            cols = slice(c * BLOCK // 2, (c + 1) * BLOCK // 2)
+            nc.sync.dma_start(out=w_words[:].bitcast(I32)[:, :, cols], in_=words_dram[:, :, cols])
+
+        load_x(0, 1)
+        load_w_block(0)
+        for quadrant in range(4):
+            nc.sync.dma_start(
+                out=w_planes[32 * quadrant : 32 * quadrant + 4].bitcast(I32),
+                in_=scales_dram[4 * quadrant : 4 * quadrant + 4],
+            )
+        nc.sync.dma_start(out=tables[:, 0], in_=cos_rows)
+        nc.sync.dma_start(out=sin_sb[:], in_=sin_rows)
+        for j in range(1, GROUP):
+            load_x(j, 1)
+        for c in (4, 1, 2, 5, 3):
+            load_w_block(c)
+        for group in range(1, GROUPS):
+            load_x(group * GROUP, GROUP)
+
+        nc.vector.tensor_copy(out=tables[:, 1, :, 0:HALF], in_=sin_sb[:, :, HALF:D])
+        nc.vector.tensor_copy(out=tables[:, 1, :, HALF:D], in_=sin_sb[:, :, 0:HALF])
+
+        def quantise_tile(j):
+            x_words = x_sb[:, j, :].bitcast(F32)
+            flipped = psum_x.tile([P, PASSES, 2, P], F32)
+            for g in range(PASSES):
+                for u in range(2):
+                    nc.tensor.transpose(
+                        flipped[:, g, u, :],
+                        x_words[:, g * WORDS + u : (g + 1) * WORDS : 2],
+                        ident[:],
+                    )
+            grouped = stage.tile([P, PASSES, P, 2], F32, align_bytes=64)
+            nc.scalar.copy(out=grouped[:], in_=flipped[:].rearrange("p g u m -> p g m u"))
+            nc.vector.quantize_mx(
+                out=x_codes[:, j, :].bitcast(FP8X4),
+                scales=x_planes[:, j, :],
+                in_=grouped[:].rearrange("p g m u -> p (g m u)").bitcast(BF16),
+            )
+
+        def project(pool, j, c):
+            bank = pool.tile([P, BLOCK], F32)
+            for g in range(PASSES):
+                nc.tensor.matmul_mx(
+                    out=bank[:],
+                    lhsT=x_codes[:, j, g * P : (g + 1) * P].bitcast(FP8X4),
+                    lhsT_scale=x_planes[:, j, g * P : (g + 1) * P],
+                    rhs=w_words[:, g, 2 * c * BLOCK : 2 * (c + 1) * BLOCK].bitcast(FP4X4),
+                    rhs_scale=w_planes[:, g, c * BLOCK : (c + 1) * BLOCK],
+                    start=(g == 0),
+                    stop=(g == PASSES - 1),
+                )
+            return bank[:].rearrange("p (h d) -> p h d", d=D)
+
+        def store(c, first, count, result):
+            heads = slice((c % 2) * BLOCK_HEADS, (c % 2 + 1) * BLOCK_HEADS)
+            rows = outs[c // 2][0, heads].rearrange("h (p j) d -> p h j d", j=TILES)
+            nc.sync.dma_start(out=rows[:, :, first : first + count, :], in_=result)
+
+        def add_halves(engine, straight, crossed):
+            engine.tensor_tensor(
+                out=straight[:, :, :, 0:HALF],
+                in0=straight[:, :, :, 0:HALF],
+                in1=crossed[:, :, :, HALF:D],
+                op=ALU.subtract,
+            )
+            engine.tensor_tensor(
+                out=straight[:, :, :, HALF:D],
+                in0=straight[:, :, :, HALF:D],
+                in1=crossed[:, :, :, 0:HALF],
+                op=ALU.add,
+            )
+
+        def rotate_block(group, c, last):
+            products = rotated.tile([P, 2, BLOCK_HEADS, GROUP, D], F32)
+            for i in range(GROUP):
+                j = group * GROUP + i
+                bank = project(psum_qk, j, c)
+                nc.vector.tensor_tensor(
+                    out=products[:, :, :, i, :],
+                    in0=bank.unsqueeze(1).to_broadcast([P, 2, BLOCK_HEADS, D]),
+                    in1=tables[:, :, j, :].unsqueeze(2).to_broadcast([P, 2, BLOCK_HEADS, D]),
+                    op=ALU.mult,
+                )
+                if last:
+                    one = slice(i, i + 1)
+                    add_halves(nc.vector, products[:, 0, :, one, :], products[:, 1, :, one, :])
+                    store(c, j, 1, products[:, 0, :, one, :])
+            if not last:
+                add_halves(nc.gpsimd, products[:, 0], products[:, 1])
+                store(c, group * GROUP, GROUP, products[:, 0])
+
+        def copy_block(group, c):
+            plain = copied.tile([P, BLOCK_HEADS, GROUP, D], F32)
+            for i in range(GROUP):
+                bank = project(psum_v, group * GROUP + i, c)
+                nc.scalar.copy(out=plain[:, :, i, :], in_=bank)
+            store(c, group * GROUP, GROUP, plain[:])
+
+        for j in range(GROUP):
+            quantise_tile(j)
+        for group in range(GROUPS):
+            for third in range(2):
+                rotate_block(group, 2 * third, False)
+                copy_block(group, 4 + third)
+                rotate_block(group, 2 * third + 1, group == GROUPS - 1 and third == 1)
+                if third == 0 and group + 1 < GROUPS:
+                    for j in range((group + 1) * GROUP, (group + 2) * GROUP):
+                        quantise_tile(j)

@@ -45,8 +45,8 @@ def tile_swaattention_pa_kernel(
     with ExitStack() as ctx:
         keep = ctx.enter_context(tc.tile_pool(name="keep", bufs=1))
         stage = ctx.enter_context(tc.tile_pool(name="stage", bufs=3))
-        rotated = ctx.enter_context(tc.tile_pool(name="rotated", bufs=4))
-        copied = ctx.enter_context(tc.tile_pool(name="copied", bufs=3))
+        rotated = ctx.enter_context(tc.tile_pool(name="rotated", bufs=6))
+        copied = ctx.enter_context(tc.tile_pool(name="copied", bufs=4))
         psum_x = ctx.enter_context(tc.psum_pool(name="psum_x", bufs=2))
         psum_qk = ctx.enter_context(tc.psum_pool(name="psum_qk", bufs=4))
         psum_v = ctx.enter_context(tc.psum_pool(name="psum_v", bufs=2))
@@ -123,10 +123,10 @@ def tile_swaattention_pa_kernel(
                 )
             return bank[:].rearrange("p (h d) -> p h d", d=D)
 
-        def store(c, first, count, result):
+        def store(queue, c, first, count, result):
             heads = slice((c % 2) * BLOCK_HEADS, (c % 2 + 1) * BLOCK_HEADS)
             rows = outs[c // 2][0, heads].rearrange("h (p j) d -> p h j d", j=TILES)
-            nc.sync.dma_start(out=rows[:, :, first : first + count, :], in_=result)
+            queue.dma_start(out=rows[:, :, first : first + count, :], in_=result)
 
         def add_halves(engine, straight, crossed):
             engine.tensor_tensor(
@@ -156,17 +156,17 @@ def tile_swaattention_pa_kernel(
                 if last:
                     one = slice(i, i + 1)
                     add_halves(nc.vector, products[:, 0, :, one, :], products[:, 1, :, one, :])
-                    store(c, j, 1, products[:, 0, :, one, :])
+                    store(nc.sync, c, j, 1, products[:, 0, :, one, :])
             if not last:
                 add_halves(nc.gpsimd, products[:, 0], products[:, 1])
-                store(c, group * GROUP, GROUP, products[:, 0])
+                store(nc.sync, c, group * GROUP, GROUP, products[:, 0])
 
         def copy_block(group, c):
             plain = copied.tile([P, BLOCK_HEADS, GROUP, D], F32)
             for i in range(GROUP):
                 bank = project(psum_v, group * GROUP + i, c)
                 nc.scalar.copy(out=plain[:, :, i, :], in_=bank)
-            store(c, group * GROUP, GROUP, plain[:])
+            store(nc.scalar, c, group * GROUP, GROUP, plain[:])
 
         for j in range(GROUP):
             quantise_tile(j)

@@ -48,8 +48,8 @@ def tile_swaattention_pa_kernel(
         rotated = ctx.enter_context(tc.tile_pool(name="rotated", bufs=6))
         copied = ctx.enter_context(tc.tile_pool(name="copied", bufs=4))
         psum_x = ctx.enter_context(tc.psum_pool(name="psum_x", bufs=2))
-        psum_qk = ctx.enter_context(tc.psum_pool(name="psum_qk", bufs=4))
-        psum_v = ctx.enter_context(tc.psum_pool(name="psum_v", bufs=2))
+        psum_qk = ctx.enter_context(tc.psum_pool(name="psum_qk", bufs=5))
+        psum_v = ctx.enter_context(tc.psum_pool(name="psum_v", bufs=1))
 
         x_sb = keep.tile([P, TILES, C], BF16)
         w_words = keep.tile([P, PASSES, 2 * 3 * C], U8, align_bytes=64)
@@ -142,39 +142,61 @@ def tile_swaattention_pa_kernel(
                 op=ALU.add,
             )
 
-        def rotate_block(group, c, last):
-            products = rotated.tile([P, 2, BLOCK_HEADS, GROUP, D], F32)
-            for i in range(GROUP):
-                j = group * GROUP + i
-                bank = project(psum_qk, j, c)
-                nc.vector.tensor_tensor(
-                    out=products[:, :, :, i, :],
-                    in0=bank.unsqueeze(1).to_broadcast([P, 2, BLOCK_HEADS, D]),
-                    in1=tables[:, :, j, :].unsqueeze(2).to_broadcast([P, 2, BLOCK_HEADS, D]),
-                    op=ALU.mult,
-                )
-                if last:
-                    one = slice(i, i + 1)
-                    add_halves(nc.vector, products[:, 0, :, one, :], products[:, 1, :, one, :])
-                    store(nc.sync, c, j, 1, products[:, 0, :, one, :])
-            if not last:
+        def rope_bank(products, group, c, i, last):
+            j = group * GROUP + i
+            bank = project(psum_qk, j, c)
+            nc.vector.tensor_tensor(
+                out=products[:, :, :, i, :],
+                in0=bank.unsqueeze(1).to_broadcast([P, 2, BLOCK_HEADS, D]),
+                in1=tables[:, :, j, :].unsqueeze(2).to_broadcast([P, 2, BLOCK_HEADS, D]),
+                op=ALU.mult,
+            )
+            if last:
+                one = slice(i, i + 1)
+                add_halves(nc.vector, products[:, 0, :, one, :], products[:, 1, :, one, :])
+                store(nc.sync, c, j, 1, products[:, 0, :, one, :])
+            elif i == GROUP - 1:
                 add_halves(nc.gpsimd, products[:, 0], products[:, 1])
                 store(nc.sync, c, group * GROUP, GROUP, products[:, 0])
 
-        def copy_block(group, c):
-            plain = copied.tile([P, BLOCK_HEADS, GROUP, D], F32)
-            for i in range(GROUP):
-                bank = project(psum_v, group * GROUP + i, c)
-                nc.scalar.copy(out=plain[:, :, i, :], in_=bank)
-            store(nc.scalar, c, group * GROUP, GROUP, plain[:])
+        def v_bank(plain, group, c, i):
+            bank = project(psum_v, group * GROUP + i, c)
+            nc.scalar.copy(out=plain[:, :, i, :], in_=bank)
+            if i == GROUP - 1:
+                store(nc.scalar, c, group * GROUP, GROUP, plain[:])
 
-        for j in range(GROUP):
-            quantise_tile(j)
+        ctx.enter_context(tc.manual_schedule(engines={mybir.EngineType.PE}))
+        def other_work(group):
+            plan = {}
+            if group == 0:
+                plan[0] = ("x", 2)
+                plan[1] = ("x", 3)
+                for n in range(GROUP):
+                    plan[GROUP + 3 * n] = ("v", 2 * n)
+                    plan[GROUP + 3 * n + 1] = ("x", GROUP + n)
+                    plan[GROUP + 3 * n + 2] = ("v", 2 * n + 1)
+            else:
+                for n in range(2 * GROUP):
+                    plan[2 * n + 1] = ("v", n)
+                if group + 1 < GROUPS:
+                    for n in range(GROUP):
+                        plan[4 * n] = ("x", (group + 1) * GROUP + n)
+            return plan
+
+        quantise_tile(0)
+        quantise_tile(1)
         for group in range(GROUPS):
-            for third in range(2):
-                rotate_block(group, 2 * third, False)
-                copy_block(group, 4 + third)
-                rotate_block(group, 2 * third + 1, group == GROUPS - 1 and third == 1)
-                if third == 0 and group + 1 < GROUPS:
-                    for j in range((group + 1) * GROUP, (group + 2) * GROUP):
-                        quantise_tile(j)
+            plan = other_work(group)
+            for k in range(4 * GROUP):
+                c, i = divmod(k, GROUP)
+                if i == 0:
+                    products = rotated.tile([P, 2, BLOCK_HEADS, GROUP, D], F32)
+                rope_bank(products, group, c, i, group == GROUPS - 1 and c == 3)
+                kind, n = plan.get(k, ("", 0))
+                if kind == "x":
+                    quantise_tile(n)
+                if kind == "v":
+                    c_v, i_v = divmod(n, GROUP)
+                    if i_v == 0:
+                        plain = copied.tile([P, BLOCK_HEADS, GROUP, D], F32)
+                    v_bank(plain, group, 4 + c_v, i_v)

@@ -27,6 +27,8 @@ BLOCK_HEADS = 4
 BLOCK = BLOCK_HEADS * D
 BLOCKS = 3 * C // BLOCK
 
+WARM_UP = 5
+
 FLOPS = 2 * T * C * 3 * C
 
 
@@ -52,14 +54,18 @@ def tile_swaattention_pa_kernel(
         psum_v = ctx.enter_context(tc.psum_pool(name="psum_v", bufs=1))
 
         x_sb = keep.tile([P, TILES, C], BF16)
-        w_words = keep.tile([P, PASSES, 2 * 3 * C], U8, align_bytes=64)
+        w_words = keep.tile([P, BLOCKS, PASSES, 2 * BLOCK], U8, align_bytes=64)
         w_planes = keep.tile([P, PASSES, 3 * C], U8, align_bytes=64)
-        tables = keep.tile([P, 2, TILES, D], BF16)
-        sin_sb = keep.tile([P, TILES, D], BF16)
+        tables_head = keep.tile([P, 2, GROUP, D], BF16)
+        tables_rest = keep.tile([P, 2, TILES - GROUP, D], BF16)
+        sin_head = keep.tile([P, GROUP, D], BF16)
+        sin_rest = keep.tile([P, TILES - GROUP, D], BF16)
         ident = keep.tile([P, P], F32)
+        warm = keep.tile([P, BLOCK], BF16)
         x_codes = keep.tile([P, TILES, PASSES * P], U32, align_bytes=64)
         x_planes = keep.tile([P, TILES, PASSES * P], U8, align_bytes=64)
 
+        nc.gpsimd.memset(warm[:], 0.0)
         nc.vector.memset(w_planes[:].bitcast(I32), 0)
         make_identity(nc, ident[:])
 
@@ -70,28 +76,37 @@ def tile_swaattention_pa_kernel(
 
         def load_w_block(c):
             cols = slice(c * BLOCK // 2, (c + 1) * BLOCK // 2)
-            nc.sync.dma_start(out=w_words[:].bitcast(I32)[:, :, cols], in_=words_dram[:, :, cols])
+            nc.sync.dma_start(out=w_words[:, c].bitcast(I32), in_=words_dram[:, :, cols])
+
+        def load_tables(tables, sin_sb, tiles):
+            nc.sync.dma_start(out=tables[:, 0], in_=cos_rows[:, tiles, :])
+            nc.sync.dma_start(out=sin_sb[:], in_=sin_rows[:, tiles, :])
+
+        def swap_sin(tables, sin_sb):
+            nc.vector.tensor_copy(out=tables[:, 1, :, 0:HALF], in_=sin_sb[:, :, HALF:D])
+            nc.vector.tensor_copy(out=tables[:, 1, :, HALF:D], in_=sin_sb[:, :, 0:HALF])
 
         load_x(0, 1)
+        load_x(1, 1)
         load_w_block(0)
         for quadrant in range(4):
             nc.sync.dma_start(
                 out=w_planes[32 * quadrant : 32 * quadrant + 4].bitcast(I32),
                 in_=scales_dram[4 * quadrant : 4 * quadrant + 4],
             )
-        nc.sync.dma_start(out=tables[:, 0], in_=cos_rows)
-        nc.sync.dma_start(out=sin_sb[:], in_=sin_rows)
-        for j in range(1, GROUP):
-            load_x(j, 1)
-        for c in (4, 1, 2, 5, 3):
-            load_w_block(c)
-        for group in range(1, GROUPS):
-            load_x(group * GROUP, GROUP)
+        load_tables(tables_head, sin_head, slice(0, GROUP))
+        load_x(2, 1)
+        load_x(3, 1)
+        load_w_block(1)
+        load_w_block(4)
+        load_w_block(2)
+        load_x(GROUP, GROUP)
+        load_tables(tables_rest, sin_rest, slice(GROUP, TILES))
+        load_w_block(5)
+        load_w_block(3)
+        load_x(2 * GROUP, GROUP)
 
-        nc.vector.tensor_copy(out=tables[:, 1, :, 0:HALF], in_=sin_sb[:, :, HALF:D])
-        nc.vector.tensor_copy(out=tables[:, 1, :, HALF:D], in_=sin_sb[:, :, 0:HALF])
-
-        def quantise_tile(j):
+        def flip_tile(j):
             x_words = x_sb[:, j, :].bitcast(F32)
             flipped = psum_x.tile([P, PASSES, 2, P], F32)
             for g in range(PASSES):
@@ -103,6 +118,9 @@ def tile_swaattention_pa_kernel(
                     )
             grouped = stage.tile([P, PASSES, P, 2], F32, align_bytes=64)
             nc.scalar.copy(out=grouped[:], in_=flipped[:].rearrange("p g u m -> p g m u"))
+            return grouped
+
+        def quantise_tile(j, grouped):
             nc.vector.quantize_mx(
                 out=x_codes[:, j, :].bitcast(FP8X4),
                 scales=x_planes[:, j, :],
@@ -116,7 +134,7 @@ def tile_swaattention_pa_kernel(
                     out=bank[:],
                     lhsT=x_codes[:, j, g * P : (g + 1) * P].bitcast(FP8X4),
                     lhsT_scale=x_planes[:, j, g * P : (g + 1) * P],
-                    rhs=w_words[:, g, 2 * c * BLOCK : 2 * (c + 1) * BLOCK].bitcast(FP4X4),
+                    rhs=w_words[:, c, g, :].bitcast(FP4X4),
                     rhs_scale=w_planes[:, g, c * BLOCK : (c + 1) * BLOCK],
                     start=(g == 0),
                     stop=(g == PASSES - 1),
@@ -142,22 +160,28 @@ def tile_swaattention_pa_kernel(
                 op=ALU.add,
             )
 
-        def rope_bank(products, group, c, i, last):
+        def table_of(j):
+            return tables_head[:, :, j, :] if j < GROUP else tables_rest[:, :, j - GROUP, :]
+
+        def rope_bank(products, group, c, i):
             j = group * GROUP + i
             bank = project(psum_qk, j, c)
             nc.vector.tensor_tensor(
                 out=products[:, :, :, i, :],
                 in0=bank.unsqueeze(1).to_broadcast([P, 2, BLOCK_HEADS, D]),
-                in1=tables[:, :, j, :].unsqueeze(2).to_broadcast([P, 2, BLOCK_HEADS, D]),
+                in1=table_of(j).unsqueeze(2).to_broadcast([P, 2, BLOCK_HEADS, D]),
                 op=ALU.mult,
             )
-            if last:
-                one = slice(i, i + 1)
-                add_halves(nc.vector, products[:, 0, :, one, :], products[:, 1, :, one, :])
-                store(nc.sync, c, j, 1, products[:, 0, :, one, :])
-            elif i == GROUP - 1:
-                add_halves(nc.gpsimd, products[:, 0], products[:, 1])
-                store(nc.sync, c, group * GROUP, GROUP, products[:, 0])
+
+        def finish(engine, products, group, c, first, count, stored):
+            some = slice(first, first + count)
+            add_halves(engine, products[:, 0, :, some, :], products[:, 1, :, some, :])
+            if stored:
+                begin = first + count - stored
+                store(
+                    nc.sync, c, group * GROUP + begin, stored,
+                    products[:, 0, :, begin : begin + stored, :],
+                )
 
         def v_bank(plain, group, c, i):
             bank = project(psum_v, group * GROUP + i, c)
@@ -165,38 +189,59 @@ def tile_swaattention_pa_kernel(
             if i == GROUP - 1:
                 store(nc.scalar, c, group * GROUP, GROUP, plain[:])
 
-        ctx.enter_context(tc.manual_schedule(engines={mybir.EngineType.PE}))
-        def other_work(group):
-            plan = {}
-            if group == 0:
-                plan[0] = ("x", 2)
-                plan[1] = ("x", 3)
+        behind = {}
+        for s in range(TILES * 4 + 2):
+            behind[s] = []
+        behind[0].extend([("flip", 2), ("quantise", 2)])
+        behind[1].extend([("flip", 3), ("quantise", 3)])
+        for n in range(GROUP):
+            behind[GROUP + 3 * n].append(("v", 2 * n))
+            behind[GROUP + 3 * n + 1].append(("flip", GROUP + n))
+            behind[GROUP + 3 * n + 2].append(("v", 2 * n + 1))
+            behind[GROUP + 3 * n + 3].append(("quantise", GROUP + n))
+        for group in range(1, GROUPS):
+            for n in range(2 * GROUP):
+                behind[16 * group + 2 * n + 1].append(("v", n))
+            if group + 1 < GROUPS:
                 for n in range(GROUP):
-                    plan[GROUP + 3 * n] = ("v", 2 * n)
-                    plan[GROUP + 3 * n + 1] = ("x", GROUP + n)
-                    plan[GROUP + 3 * n + 2] = ("v", 2 * n + 1)
-            else:
-                for n in range(2 * GROUP):
-                    plan[2 * n + 1] = ("v", n)
-                if group + 1 < GROUPS:
-                    for n in range(GROUP):
-                        plan[4 * n] = ("x", (group + 1) * GROUP + n)
-            return plan
+                    behind[16 * group + 4 * n].append(("flip", (group + 1) * GROUP + n))
+                    behind[16 * group + 4 * n + 2].append(("quantise", (group + 1) * GROUP + n))
 
-        quantise_tile(0)
-        quantise_tile(1)
+        ctx.enter_context(
+            tc.manual_schedule(engines={mybir.EngineType.PE, mybir.EngineType.DVE})
+        )
+        bank = psum_qk.tile([P, BLOCK], F32)
+        for n in range(WARM_UP):
+            nc.tensor.matmul(bank[:], lhsT=warm[:, 0:P], rhs=warm[:], start=True, stop=True)
+
+        flipped_tiles = {}
+        flipped_tiles[0] = flip_tile(0)
+        flipped_tiles[1] = flip_tile(1)
+        quantise_tile(0, flipped_tiles[0])
+        quantise_tile(1, flipped_tiles[1])
+        swap_sin(tables_head, sin_head)
         for group in range(GROUPS):
-            plan = other_work(group)
             for k in range(4 * GROUP):
                 c, i = divmod(k, GROUP)
+                s = 16 * group + k
                 if i == 0:
                     products = rotated.tile([P, 2, BLOCK_HEADS, GROUP, D], F32)
-                rope_bank(products, group, c, i, group == GROUPS - 1 and c == 3)
-                kind, n = plan.get(k, ("", 0))
-                if kind == "x":
-                    quantise_tile(n)
-                if kind == "v":
-                    c_v, i_v = divmod(n, GROUP)
-                    if i_v == 0:
-                        plain = copied.tile([P, BLOCK_HEADS, GROUP, D], F32)
-                    v_bank(plain, group, 4 + c_v, i_v)
+                rope_bank(products, group, c, i)
+                if s >= 44:
+                    finish(nc.vector, products, group, c, i, 1, 1)
+                elif s < GROUP and i % 2 == 1:
+                    finish(nc.gpsimd, products, group, c, i - 1, 2, GROUP if i == GROUP - 1 else 0)
+                elif s >= GROUP and i == GROUP - 1:
+                    finish(nc.gpsimd, products, group, c, 0, GROUP, GROUP)
+                if s == 2 * GROUP:
+                    swap_sin(tables_rest, sin_rest)
+                for kind, n in behind[s]:
+                    if kind == "flip":
+                        flipped_tiles[n] = flip_tile(n)
+                    if kind == "quantise":
+                        quantise_tile(n, flipped_tiles[n])
+                    if kind == "v":
+                        c_v, i_v = divmod(n, GROUP)
+                        if i_v == 0:
+                            plain = copied.tile([P, BLOCK_HEADS, GROUP, D], F32)
+                        v_bank(plain, group, 4 + c_v, i_v)

@@ -28,6 +28,7 @@ BLOCK = BLOCK_HEADS * D
 BLOCKS = 3 * C // BLOCK
 
 WARM_UP = 5
+LAST_BANK = 4 * TILES - 1
 
 FLOPS = 2 * T * C * 3 * C
 
@@ -227,14 +228,18 @@ def tile_swaattention_pa_kernel(
                 if i == 0:
                     products = rotated.tile([P, 2, BLOCK_HEADS, GROUP, D], F32)
                 rope_bank(products, group, c, i)
-                if s >= 44:
-                    finish(nc.vector, products, group, c, i, 1, 1)
+                if s == LAST_BANK:
+                    for tile in range(GROUP):
+                        finish(nc.vector, products, group, c, tile, 1, 1)
+                elif s > LAST_BANK - GROUP:
+                    pass
                 elif s < GROUP and i % 2 == 1:
                     finish(nc.gpsimd, products, group, c, i - 1, 2, GROUP if i == GROUP - 1 else 0)
                 elif s >= GROUP and i == GROUP - 1:
                     finish(nc.gpsimd, products, group, c, 0, GROUP, GROUP)
                 if s == 2 * GROUP:
-                    swap_sin(tables_rest, sin_rest)
+                    nc.scalar.copy(out=tables_rest[:, 1, :, 0:HALF], in_=sin_rest[:, :, HALF:D])
+                    nc.scalar.copy(out=tables_rest[:, 1, :, HALF:D], in_=sin_rest[:, :, 0:HALF])
                 for kind, n in behind[s]:
                     if kind == "flip":
                         flipped_tiles[n] = flip_tile(n)

@@ -29,6 +29,7 @@ BLOCKS = 3 * C // BLOCK
 
 WARM_UP = 5
 LAST_BANK = 4 * TILES - 1
+VECTOR_ADDS_BANK = 31
 
 FLOPS = 2 * T * C * 3 * C
 
@@ -107,7 +108,7 @@ def tile_swaattention_pa_kernel(
         load_w_block(3)
         load_x(2 * GROUP, GROUP)
 
-        def flip_tile(j):
+        def flip_tile(j, grouped, place):
             x_words = x_sb[:, j, :].bitcast(F32)
             flipped = psum_x.tile([P, PASSES, 2, P], F32)
             for g in range(PASSES):
@@ -117,15 +118,13 @@ def tile_swaattention_pa_kernel(
                         x_words[:, g * WORDS + u : (g + 1) * WORDS : 2],
                         ident[:],
                     )
-            grouped = stage.tile([P, PASSES, P, 2], F32, align_bytes=64)
-            nc.scalar.copy(out=grouped[:], in_=flipped[:].rearrange("p g u m -> p g m u"))
-            return grouped
+            nc.scalar.copy(out=grouped[:, place], in_=flipped[:].rearrange("p g u m -> p g m u"))
 
-        def quantise_tile(j, grouped):
+        def quantise_tiles(first, count, grouped):
             nc.vector.quantize_mx(
-                out=x_codes[:, j, :].bitcast(FP8X4),
-                scales=x_planes[:, j, :],
-                in_=grouped[:].rearrange("p g m u -> p (g m u)").bitcast(BF16),
+                out=x_codes[:, first : first + count, :].rearrange("p j c -> p (j c)").bitcast(FP8X4),
+                scales=x_planes[:, first : first + count, :].rearrange("p j c -> p (j c)"),
+                in_=grouped[:].rearrange("p j g m u -> p (j g m u)").bitcast(BF16),
             )
 
         def project(pool, j, c):
@@ -191,22 +190,22 @@ def tile_swaattention_pa_kernel(
                 store(nc.scalar, c, group * GROUP, GROUP, plain[:])
 
         behind = {}
-        for s in range(TILES * 4 + 2):
+        for s in range(4 * TILES):
             behind[s] = []
         behind[0].extend([("flip", 2), ("quantise", 2)])
         behind[1].extend([("flip", 3), ("quantise", 3)])
         for n in range(GROUP):
-            behind[GROUP + 3 * n].append(("v", 2 * n))
-            behind[GROUP + 3 * n + 1].append(("flip", GROUP + n))
-            behind[GROUP + 3 * n + 2].append(("v", 2 * n + 1))
-            behind[GROUP + 3 * n + 3].append(("quantise", GROUP + n))
+            behind[GROUP + 2 * n].append(("v", n))
+            behind[GROUP + 2 * n + 1].append(("flip", GROUP + n))
+            behind[3 * GROUP + n].append(("v", GROUP + n))
+        behind[3 * GROUP + 1].append(("quantise", GROUP))
         for group in range(1, GROUPS):
             for n in range(2 * GROUP):
                 behind[16 * group + 2 * n + 1].append(("v", n))
             if group + 1 < GROUPS:
                 for n in range(GROUP):
-                    behind[16 * group + 4 * n].append(("flip", (group + 1) * GROUP + n))
-                    behind[16 * group + 4 * n + 2].append(("quantise", (group + 1) * GROUP + n))
+                    behind[16 * group + 2 * n].append(("flip", (group + 1) * GROUP + n))
+                behind[16 * group + 2 * GROUP].append(("quantise", (group + 1) * GROUP))
 
         ctx.enter_context(
             tc.manual_schedule(engines={mybir.EngineType.PE, mybir.EngineType.DVE})
@@ -215,11 +214,10 @@ def tile_swaattention_pa_kernel(
         for n in range(WARM_UP):
             nc.tensor.matmul(bank[:], lhsT=warm[:, 0:P], rhs=warm[:], start=True, stop=True)
 
-        flipped_tiles = {}
-        flipped_tiles[0] = flip_tile(0)
-        flipped_tiles[1] = flip_tile(1)
-        quantise_tile(0, flipped_tiles[0])
-        quantise_tile(1, flipped_tiles[1])
+        for j in range(2):
+            grouped = stage.tile([P, 1, PASSES, P, 2], F32, align_bytes=64)
+            flip_tile(j, grouped, 0)
+            quantise_tiles(j, 1, grouped)
         swap_sin(tables_head, sin_head)
         for group in range(GROUPS):
             for k in range(4 * GROUP):
@@ -233,6 +231,8 @@ def tile_swaattention_pa_kernel(
                         finish(nc.vector, products, group, c, tile, 1, 1)
                 elif s > LAST_BANK - GROUP:
                     pass
+                elif s == VECTOR_ADDS_BANK:
+                    finish(nc.vector, products, group, c, 0, GROUP, GROUP)
                 elif s < GROUP and i % 2 == 1:
                     finish(nc.gpsimd, products, group, c, i - 1, 2, GROUP if i == GROUP - 1 else 0)
                 elif s >= GROUP and i == GROUP - 1:
@@ -242,9 +242,13 @@ def tile_swaattention_pa_kernel(
                     nc.scalar.copy(out=tables_rest[:, 1, :, HALF:D], in_=sin_rest[:, :, 0:HALF])
                 for kind, n in behind[s]:
                     if kind == "flip":
-                        flipped_tiles[n] = flip_tile(n)
+                        if n < GROUP or n % GROUP == 0:
+                            grouped = stage.tile(
+                                [P, 1 if n < GROUP else GROUP, PASSES, P, 2], F32, align_bytes=64
+                            )
+                        flip_tile(n, grouped, 0 if n < GROUP else n % GROUP)
                     if kind == "quantise":
-                        quantise_tile(n, flipped_tiles[n])
+                        quantise_tiles(n, 1 if n < GROUP else GROUP, grouped)
                     if kind == "v":
                         c_v, i_v = divmod(n, GROUP)
                         if i_v == 0:

@@ -29,7 +29,7 @@ BLOCKS = 3 * C // BLOCK
 
 WARM_UP = 5
 LAST_BANK = 4 * TILES - 1
-VECTOR_ADDS_BANK = 31
+VECTOR_ADDS_EVERY = 3 * GROUP
 
 FLOPS = 2 * T * C * 3 * C
 
@@ -231,7 +231,7 @@ def tile_swaattention_pa_kernel(
                         finish(nc.vector, products, group, c, tile, 1, 1)
                 elif s > LAST_BANK - GROUP:
                     pass
-                elif s == VECTOR_ADDS_BANK:
+                elif (s + 1) % VECTOR_ADDS_EVERY == 0:
                     finish(nc.vector, products, group, c, 0, GROUP, GROUP)
                 elif s < GROUP and i % 2 == 1:
                     finish(nc.gpsimd, products, group, c, i - 1, 2, GROUP if i == GROUP - 1 else 0)

@@ -29,7 +29,7 @@ BLOCKS = 3 * C // BLOCK
 
 WARM_UP = 5
 LAST_BANK = 4 * TILES - 1
-VECTOR_ADDS_EVERY = 3 * GROUP
+VECTOR_ADDS_EVERY = 4 * GROUP
 
 FLOPS = 2 * T * C * 3 * C
 
@@ -57,7 +57,8 @@ def tile_swaattention_pa_kernel(
 
         x_sb = keep.tile([P, TILES, C], BF16)
         w_words = keep.tile([P, BLOCKS, PASSES, 2 * BLOCK], U8, align_bytes=64)
-        w_planes = keep.tile([P, PASSES, 3 * C], U8, align_bytes=64)
+        w_planes_first = keep.tile([P, PASSES, BLOCK], U8, align_bytes=64)
+        w_planes_rest = keep.tile([P, PASSES, 3 * C - BLOCK], U8, align_bytes=64)
         tables_head = keep.tile([P, 2, GROUP, D], BF16)
         tables_rest = keep.tile([P, 2, TILES - GROUP, D], BF16)
         sin_head = keep.tile([P, GROUP, D], BF16)
@@ -68,7 +69,8 @@ def tile_swaattention_pa_kernel(
         x_planes = keep.tile([P, TILES, PASSES * P], U8, align_bytes=64)
 
         nc.gpsimd.memset(warm[:], 0.0)
-        nc.vector.memset(w_planes[:].bitcast(I32), 0)
+        nc.vector.memset(w_planes_first[:].bitcast(I32), 0)
+        nc.vector.memset(w_planes_rest[:].bitcast(I32), 0)
         make_identity(nc, ident[:])
 
         def load_x(first, count):
@@ -79,6 +81,13 @@ def tile_swaattention_pa_kernel(
         def load_w_block(c):
             cols = slice(c * BLOCK // 2, (c + 1) * BLOCK // 2)
             nc.sync.dma_start(out=w_words[:, c].bitcast(I32), in_=words_dram[:, :, cols])
+
+        def load_scales(planes, cols):
+            for quadrant in range(4):
+                nc.sync.dma_start(
+                    out=planes[32 * quadrant : 32 * quadrant + 4].bitcast(I32),
+                    in_=scales_dram[4 * quadrant : 4 * quadrant + 4, :, cols],
+                )
 
         def load_tables(tables, sin_sb, tiles):
             nc.sync.dma_start(out=tables[:, 0], in_=cos_rows[:, tiles, :])
@@ -91,14 +100,11 @@ def tile_swaattention_pa_kernel(
         load_x(0, 1)
         load_x(1, 1)
         load_w_block(0)
-        for quadrant in range(4):
-            nc.sync.dma_start(
-                out=w_planes[32 * quadrant : 32 * quadrant + 4].bitcast(I32),
-                in_=scales_dram[4 * quadrant : 4 * quadrant + 4],
-            )
+        load_scales(w_planes_first, slice(0, BLOCK // 4))
         load_tables(tables_head, sin_head, slice(0, GROUP))
         load_x(2, 1)
         load_x(3, 1)
+        load_scales(w_planes_rest, slice(BLOCK // 4, 3 * C // 4))
         load_w_block(1)
         load_w_block(4)
         load_w_block(2)
@@ -135,7 +141,11 @@ def tile_swaattention_pa_kernel(
                     lhsT=x_codes[:, j, g * P : (g + 1) * P].bitcast(FP8X4),
                     lhsT_scale=x_planes[:, j, g * P : (g + 1) * P],
                     rhs=w_words[:, c, g, :].bitcast(FP4X4),
-                    rhs_scale=w_planes[:, g, c * BLOCK : (c + 1) * BLOCK],
+                    rhs_scale=(
+                        w_planes_first[:, g, :]
+                        if c == 0
+                        else w_planes_rest[:, g, (c - 1) * BLOCK : c * BLOCK]
+                    ),
                     start=(g == 0),
                     stop=(g == PASSES - 1),
                 )

@@ -29,7 +29,6 @@ BLOCKS = 3 * C // BLOCK
 
 WARM_UP = 5
 LAST_BANK = 4 * TILES - 1
-VECTOR_ADDS_EVERY = 4 * GROUP
 
 FLOPS = 2 * T * C * 3 * C
 
@@ -178,8 +177,8 @@ def tile_swaattention_pa_kernel(
             bank = project(psum_qk, j, c)
             nc.vector.tensor_tensor(
                 out=products[:, :, :, i, :],
-                in0=bank.unsqueeze(1).to_broadcast([P, 2, BLOCK_HEADS, D]),
-                in1=table_of(j).unsqueeze(2).to_broadcast([P, 2, BLOCK_HEADS, D]),
+                in0=table_of(j).unsqueeze(2).to_broadcast([P, 2, BLOCK_HEADS, D]),
+                in1=bank.unsqueeze(1).to_broadcast([P, 2, BLOCK_HEADS, D]),
                 op=ALU.mult,
             )
 
@@ -209,13 +208,13 @@ def tile_swaattention_pa_kernel(
             behind[GROUP + 2 * n + 1].append(("flip", GROUP + n))
             behind[3 * GROUP + n].append(("v", GROUP + n))
         behind[3 * GROUP + 1].append(("quantise", GROUP))
-        for group in range(1, GROUPS):
-            for n in range(2 * GROUP):
-                behind[16 * group + 2 * n + 1].append(("v", n))
-            if group + 1 < GROUPS:
-                for n in range(GROUP):
-                    behind[16 * group + 2 * n].append(("flip", (group + 1) * GROUP + n))
-                behind[16 * group + 2 * GROUP].append(("quantise", (group + 1) * GROUP))
+        for n in range(GROUP):
+            behind[4 * GROUP + 2 * n].append(("flip", 2 * GROUP + n))
+            behind[4 * GROUP + 2 * n + 1].append(("v", 2 * GROUP + n))
+            behind[6 * GROUP + n].append(("v", 3 * GROUP + n))
+        behind[6 * GROUP].append(("quantise", 2 * GROUP))
+        for n in range(2 * GROUP):
+            behind[7 * GROUP + 2 * n].append(("v", 4 * GROUP + n))
 
         ctx.enter_context(
             tc.manual_schedule(engines={mybir.EngineType.PE, mybir.EngineType.DVE})
@@ -241,8 +240,6 @@ def tile_swaattention_pa_kernel(
                         finish(nc.vector, products, group, c, tile, 1, 1)
                 elif s > LAST_BANK - GROUP:
                     pass
-                elif (s + 1) % VECTOR_ADDS_EVERY == 0:
-                    finish(nc.vector, products, group, c, 0, GROUP, GROUP)
                 elif s < GROUP and i % 2 == 1:
                     finish(nc.gpsimd, products, group, c, i - 1, 2, GROUP if i == GROUP - 1 else 0)
                 elif s >= GROUP and i == GROUP - 1:
@@ -260,7 +257,7 @@ def tile_swaattention_pa_kernel(
                     if kind == "quantise":
                         quantise_tiles(n, 1 if n < GROUP else GROUP, grouped)
                     if kind == "v":
-                        c_v, i_v = divmod(n, GROUP)
+                        patch, i_v = divmod(n, GROUP)
                         if i_v == 0:
                             plain = copied.tile([P, BLOCK_HEADS, GROUP, D], F32)
-                        v_bank(plain, group, 4 + c_v, i_v)
+                        v_bank(plain, patch // 2, 4 + patch % 2, i_v)

@@ -50,9 +50,8 @@ def tile_swaattention_pa_kernel(
         stage = ctx.enter_context(tc.tile_pool(name="stage", bufs=3))
         rotated = ctx.enter_context(tc.tile_pool(name="rotated", bufs=6))
         copied = ctx.enter_context(tc.tile_pool(name="copied", bufs=4))
-        psum_x = ctx.enter_context(tc.psum_pool(name="psum_x", bufs=2))
-        psum_qk = ctx.enter_context(tc.psum_pool(name="psum_qk", bufs=5))
-        psum_v = ctx.enter_context(tc.psum_pool(name="psum_v", bufs=1))
+        psum_rope = ctx.enter_context(tc.psum_pool(name="psum_rope", bufs=5))
+        psum_side = ctx.enter_context(tc.psum_pool(name="psum_side", bufs=3))
 
         x_sb = keep.tile([P, TILES, C], BF16)
         w_words = keep.tile([P, BLOCKS, PASSES, 2 * BLOCK], U8, align_bytes=64)
@@ -115,7 +114,8 @@ def tile_swaattention_pa_kernel(
 
         def flip_tile(j, grouped, place):
             x_words = x_sb[:, j, :].bitcast(F32)
-            flipped = psum_x.tile([P, PASSES, 2, P], F32)
+            bank = psum_side.tile([P, BLOCK], F32)
+            flipped = bank[:].rearrange("p (g u m) -> p g u m", u=2, m=P)
             for g in range(PASSES):
                 for u in range(2):
                     nc.tensor.transpose(
@@ -123,7 +123,7 @@ def tile_swaattention_pa_kernel(
                         x_words[:, g * WORDS + u : (g + 1) * WORDS : 2],
                         ident[:],
                     )
-            nc.scalar.copy(out=grouped[:, place], in_=flipped[:].rearrange("p g u m -> p g m u"))
+            nc.scalar.copy(out=grouped[:, place], in_=flipped.rearrange("p g u m -> p g m u"))
 
         def quantise_tiles(first, count, grouped):
             nc.vector.quantize_mx(
@@ -132,8 +132,7 @@ def tile_swaattention_pa_kernel(
                 in_=grouped[:].rearrange("p j g m u -> p (j g m u)").bitcast(BF16),
             )
 
-        def project(pool, j, c):
-            bank = pool.tile([P, BLOCK], F32)
+        def project(bank, j, c):
             for g in range(PASSES):
                 nc.tensor.matmul_mx(
                     out=bank[:],
@@ -174,7 +173,8 @@ def tile_swaattention_pa_kernel(
 
         def rope_bank(products, group, c, i):
             j = group * GROUP + i
-            bank = project(psum_qk, j, c)
+            rope = psum_rope.tile([P, BLOCK], F32)
+            bank = project(rope, j, c)
             nc.vector.tensor_tensor(
                 out=products[:, :, :, i, :],
                 in0=table_of(j).unsqueeze(2).to_broadcast([P, 2, BLOCK_HEADS, D]),
@@ -193,8 +193,8 @@ def tile_swaattention_pa_kernel(
                 )
 
         def v_bank(plain, group, c, i):
-            bank = project(psum_v, group * GROUP + i, c)
-            nc.scalar.copy(out=plain[:, :, i, :], in_=bank)
+            bank = psum_side.tile([P, BLOCK], F32)
+            nc.scalar.copy(out=plain[:, :, i, :], in_=project(bank, group * GROUP + i, c))
             if i == GROUP - 1:
                 store(nc.scalar, c, group * GROUP, GROUP, plain[:])
 
@@ -219,9 +219,9 @@ def tile_swaattention_pa_kernel(
         ctx.enter_context(
             tc.manual_schedule(engines={mybir.EngineType.PE, mybir.EngineType.DVE})
         )
-        bank = psum_qk.tile([P, BLOCK], F32)
+        rope = psum_rope.tile([P, BLOCK], F32)
         for n in range(WARM_UP):
-            nc.tensor.matmul(bank[:], lhsT=warm[:, 0:P], rhs=warm[:], start=True, stop=True)
+            nc.tensor.matmul(rope[:], lhsT=warm[:, 0:P], rhs=warm[:], start=True, stop=True)
 
         for j in range(2):
             grouped = stage.tile([P, 1, PASSES, P, 2], F32, align_bytes=64)

@@ -228,17 +228,22 @@ def tile_swaattention_pa_kernel(
             flip_tile(j, grouped, 0)
             quantise_tiles(j, 1, grouped)
         swap_sin(tables_head, sin_head)
+        late = []
         for group in range(GROUPS):
             for k in range(4 * GROUP):
                 c, i = divmod(k, GROUP)
                 s = 16 * group + k
                 if i == 0:
                     products = rotated.tile([P, 2, BLOCK_HEADS, GROUP, D], F32)
+                    if s > LAST_BANK - 2 * GROUP:
+                        late.append(products)
                 rope_bank(products, group, c, i)
                 if s == LAST_BANK:
+                    for first in range(0, GROUP, 2):
+                        finish(nc.vector, late[0], group, c - 1, first, 2, 2)
                     for tile in range(GROUP):
-                        finish(nc.vector, products, group, c, tile, 1, 1)
-                elif s > LAST_BANK - GROUP:
+                        finish(nc.vector, late[1], group, c, tile, 1, 1)
+                elif s > LAST_BANK - 2 * GROUP:
                     pass
                 elif s < GROUP and i % 2 == 1:
                     finish(nc.gpsimd, products, group, c, i - 1, 2, GROUP if i == GROUP - 1 else 0)

@@ -21,14 +21,16 @@ K_PASS = 4 * P
 PASSES = C // K_PASS
 WORDS = K_PASS // 2
 TILES = T // P
-GROUP = 4
-GROUPS = TILES // GROUP
 BLOCK_HEADS = 4
 BLOCK = BLOCK_HEADS * D
 BLOCKS = 3 * C // BLOCK
+ROPE_BLOCKS = 4
+PATCH = 4
+V_PATCH = 6
 
 WARM_UP = 5
-LAST_BANK = 4 * TILES - 1
+LAST_BANK = ROPE_BLOCKS * TILES - 1
+VECTOR_PATCHES = 2
 
 FLOPS = 2 * T * C * 3 * C
 
@@ -48,19 +50,22 @@ def tile_swaattention_pa_kernel(
     with ExitStack() as ctx:
         keep = ctx.enter_context(tc.tile_pool(name="keep", bufs=1))
         stage = ctx.enter_context(tc.tile_pool(name="stage", bufs=3))
-        rotated = ctx.enter_context(tc.tile_pool(name="rotated", bufs=6))
-        copied = ctx.enter_context(tc.tile_pool(name="copied", bufs=4))
+        rotated = ctx.enter_context(tc.tile_pool(name="rotated", bufs=5))
+        summed = ctx.enter_context(tc.tile_pool(name="summed", bufs=2))
+        copied = ctx.enter_context(tc.tile_pool(name="copied", bufs=2))
         psum_rope = ctx.enter_context(tc.psum_pool(name="psum_rope", bufs=5))
         psum_side = ctx.enter_context(tc.psum_pool(name="psum_side", bufs=3))
 
         x_sb = keep.tile([P, TILES, C], BF16)
-        w_words = keep.tile([P, BLOCKS, PASSES, 2 * BLOCK], U8, align_bytes=64)
+        w_q = keep.tile([P, 2, PASSES, 2 * BLOCK], U8, align_bytes=64)
+        w_k = keep.tile([P, PASSES, 4 * BLOCK], U8, align_bytes=64)
+        w_v = keep.tile([P, PASSES, 4 * BLOCK], U8, align_bytes=64)
         w_planes_first = keep.tile([P, PASSES, BLOCK], U8, align_bytes=64)
         w_planes_rest = keep.tile([P, PASSES, 3 * C - BLOCK], U8, align_bytes=64)
-        tables_head = keep.tile([P, 2, GROUP, D], BF16)
-        tables_rest = keep.tile([P, 2, TILES - GROUP, D], BF16)
-        sin_head = keep.tile([P, GROUP, D], BF16)
-        sin_rest = keep.tile([P, TILES - GROUP, D], BF16)
+        tables_head = keep.tile([P, 2, PATCH, D], BF16)
+        tables_rest = keep.tile([P, 2, TILES - PATCH, D], BF16)
+        sin_head = keep.tile([P, PATCH, D], BF16)
+        sin_rest = keep.tile([P, TILES - PATCH, D], BF16)
         ident = keep.tile([P, P], F32)
         warm = keep.tile([P, BLOCK], BF16)
         x_codes = keep.tile([P, TILES, PASSES * P], U32, align_bytes=64)
@@ -76,9 +81,13 @@ def tile_swaattention_pa_kernel(
                 out=x_sb[:, first : first + count, :], in_=x_rows[:, first : first + count, :]
             )
 
-        def load_w_block(c):
-            cols = slice(c * BLOCK // 2, (c + 1) * BLOCK // 2)
-            nc.sync.dma_start(out=w_words[:, c].bitcast(I32), in_=words_dram[:, :, cols])
+        def load_w(words, c, blocks):
+            cols = slice(c * BLOCK // 2, (c + blocks) * BLOCK // 2)
+            nc.sync.dma_start(out=words.bitcast(I32), in_=words_dram[:, :, cols])
+
+        def load_tables(tables, sin_sb, tiles):
+            nc.sync.dma_start(out=tables[:, 0], in_=cos_rows[:, tiles, :])
+            nc.sync.dma_start(out=sin_sb[:], in_=sin_rows[:, tiles, :])
 
         def load_scales(planes, cols):
             for quadrant in range(4):
@@ -87,43 +96,33 @@ def tile_swaattention_pa_kernel(
                     in_=scales_dram[4 * quadrant : 4 * quadrant + 4, :, cols],
                 )
 
-        def load_tables(tables, sin_sb, tiles):
-            nc.sync.dma_start(out=tables[:, 0], in_=cos_rows[:, tiles, :])
-            nc.sync.dma_start(out=sin_sb[:], in_=sin_rows[:, tiles, :])
-
-        def swap_sin(tables, sin_sb):
-            nc.vector.tensor_copy(out=tables[:, 1, :, 0:HALF], in_=sin_sb[:, :, HALF:D])
-            nc.vector.tensor_copy(out=tables[:, 1, :, HALF:D], in_=sin_sb[:, :, 0:HALF])
-
         load_x(0, 1)
         load_x(1, 1)
-        load_w_block(0)
+        load_w(w_q[:, 0], 0, 1)
         load_scales(w_planes_first, slice(0, BLOCK // 4))
-        load_tables(tables_head, sin_head, slice(0, GROUP))
+        load_tables(tables_head, sin_head, slice(0, PATCH))
         load_x(2, 1)
         load_x(3, 1)
         load_scales(w_planes_rest, slice(BLOCK // 4, 3 * C // 4))
-        load_w_block(1)
-        load_w_block(4)
-        load_w_block(2)
-        load_x(GROUP, GROUP)
-        load_tables(tables_rest, sin_rest, slice(GROUP, TILES))
-        load_w_block(5)
-        load_w_block(3)
-        load_x(2 * GROUP, GROUP)
+        load_w(w_q[:, 1], 1, 1)
+        load_w(w_v[:], 4, 2)
+        load_x(PATCH, PATCH)
+        load_w(w_k[:], 2, 2)
+        load_tables(tables_rest, sin_rest, slice(PATCH, TILES))
+        load_x(2 * PATCH, PATCH)
 
         def flip_tile(j, grouped, place):
             x_words = x_sb[:, j, :].bitcast(F32)
             bank = psum_side.tile([P, BLOCK], F32)
-            flipped = bank[:].rearrange("p (g u m) -> p g u m", u=2, m=P)
+            words = bank[:].rearrange("p (g u m) -> p g u m", u=2, m=P)
             for g in range(PASSES):
                 for u in range(2):
                     nc.tensor.transpose(
-                        flipped[:, g, u, :],
+                        words[:, g, u, :],
                         x_words[:, g * WORDS + u : (g + 1) * WORDS : 2],
                         ident[:],
                     )
-            nc.scalar.copy(out=grouped[:, place], in_=flipped.rearrange("p g u m -> p g m u"))
+            nc.scalar.copy(out=grouped[:, place], in_=words.rearrange("p g u m -> p g m u"))
 
         def quantise_tiles(first, count, grouped):
             nc.vector.quantize_mx(
@@ -133,12 +132,14 @@ def tile_swaattention_pa_kernel(
             )
 
         def project(bank, j, c):
+            half = slice((c % 2) * 2 * BLOCK, (c % 2 + 1) * 2 * BLOCK)
+            words = w_q[:, c] if c < 2 else (w_k if c < 4 else w_v)[:, :, half]
             for g in range(PASSES):
                 nc.tensor.matmul_mx(
                     out=bank[:],
                     lhsT=x_codes[:, j, g * P : (g + 1) * P].bitcast(FP8X4),
                     lhsT_scale=x_planes[:, j, g * P : (g + 1) * P],
-                    rhs=w_words[:, c, g, :].bitcast(FP4X4),
+                    rhs=words[:, g, :].bitcast(FP4X4),
                     rhs_scale=(
                         w_planes_first[:, g, :]
                         if c == 0
@@ -154,67 +155,56 @@ def tile_swaattention_pa_kernel(
             rows = outs[c // 2][0, heads].rearrange("h (p j) d -> p h j d", j=TILES)
             queue.dma_start(out=rows[:, :, first : first + count, :], in_=result)
 
-        def add_halves(engine, straight, crossed):
+        def add_halves(engine, result, straight, crossed):
             engine.tensor_tensor(
-                out=straight[:, :, :, 0:HALF],
+                out=result[:, :, :, 0:HALF],
                 in0=straight[:, :, :, 0:HALF],
                 in1=crossed[:, :, :, HALF:D],
                 op=ALU.subtract,
             )
             engine.tensor_tensor(
-                out=straight[:, :, :, HALF:D],
+                out=result[:, :, :, HALF:D],
                 in0=straight[:, :, :, HALF:D],
                 in1=crossed[:, :, :, 0:HALF],
                 op=ALU.add,
             )
 
         def table_of(j):
-            return tables_head[:, :, j, :] if j < GROUP else tables_rest[:, :, j - GROUP, :]
+            return tables_head[:, :, j, :] if j < PATCH else tables_rest[:, :, j - PATCH, :]
 
-        def rope_bank(products, group, c, i):
-            j = group * GROUP + i
+        def rope_bank(products, c, j):
             rope = psum_rope.tile([P, BLOCK], F32)
             bank = project(rope, j, c)
             nc.vector.tensor_tensor(
-                out=products[:, :, :, i, :],
+                out=products[:, :, :, j % PATCH, :],
                 in0=table_of(j).unsqueeze(2).to_broadcast([P, 2, BLOCK_HEADS, D]),
                 in1=bank.unsqueeze(1).to_broadcast([P, 2, BLOCK_HEADS, D]),
                 op=ALU.mult,
             )
 
-        def finish(engine, products, group, c, first, count, stored):
-            some = slice(first, first + count)
-            add_halves(engine, products[:, 0, :, some, :], products[:, 1, :, some, :])
-            if stored:
-                begin = first + count - stored
-                store(
-                    nc.sync, c, group * GROUP + begin, stored,
-                    products[:, 0, :, begin : begin + stored, :],
-                )
-
-        def v_bank(plain, group, c, i):
+        def v_bank(plain, c, j):
             bank = psum_side.tile([P, BLOCK], F32)
-            nc.scalar.copy(out=plain[:, :, i, :], in_=project(bank, group * GROUP + i, c))
-            if i == GROUP - 1:
-                store(nc.scalar, c, group * GROUP, GROUP, plain[:])
+            nc.scalar.copy(out=plain[:, :, j % V_PATCH, :], in_=project(bank, j, c))
+            if j % V_PATCH == V_PATCH - 1:
+                store(nc.scalar, c, j - V_PATCH + 1, V_PATCH, plain[:])
+
+        patches = [(c, 0) for c in range(ROPE_BLOCKS)]
+        patches.extend((c, j) for c in range(ROPE_BLOCKS) for j in range(PATCH, TILES, PATCH))
 
         behind = {}
-        for s in range(4 * TILES):
+        for s in range(LAST_BANK + 1):
             behind[s] = []
         behind[0].extend([("flip", 2), ("quantise", 2)])
         behind[1].extend([("flip", 3), ("quantise", 3)])
-        for n in range(GROUP):
-            behind[GROUP + 2 * n].append(("v", n))
-            behind[GROUP + 2 * n + 1].append(("flip", GROUP + n))
-            behind[3 * GROUP + n].append(("v", GROUP + n))
-        behind[3 * GROUP + 1].append(("quantise", GROUP))
-        for n in range(GROUP):
-            behind[4 * GROUP + 2 * n].append(("flip", 2 * GROUP + n))
-            behind[4 * GROUP + 2 * n + 1].append(("v", 2 * GROUP + n))
-            behind[6 * GROUP + n].append(("v", 3 * GROUP + n))
-        behind[6 * GROUP].append(("quantise", 2 * GROUP))
-        for n in range(2 * GROUP):
-            behind[7 * GROUP + 2 * n].append(("v", 4 * GROUP + n))
+        for n in range(PATCH):
+            behind[5 + 2 * n].append(("flip", PATCH + n))
+            behind[12 + n].append(("flip", 2 * PATCH + n))
+        behind[13].append(("quantise", PATCH))
+        behind[17].append(("quantise", 2 * PATCH))
+        room = [6, 8, 10]
+        room.extend(range(16, LAST_BANK))
+        for n in range(2 * TILES):
+            behind[room[n]].append(("v", n))
 
         ctx.enter_context(
             tc.manual_schedule(engines={mybir.EngineType.PE, mybir.EngineType.DVE})
@@ -227,42 +217,54 @@ def tile_swaattention_pa_kernel(
             grouped = stage.tile([P, 1, PASSES, P, 2], F32, align_bytes=64)
             flip_tile(j, grouped, 0)
             quantise_tiles(j, 1, grouped)
-        swap_sin(tables_head, sin_head)
+        nc.vector.tensor_copy(out=tables_head[:, 1, :, 0:HALF], in_=sin_head[:, :, HALF:D])
+        nc.vector.tensor_copy(out=tables_head[:, 1, :, HALF:D], in_=sin_head[:, :, 0:HALF])
         late = []
-        for group in range(GROUPS):
-            for k in range(4 * GROUP):
-                c, i = divmod(k, GROUP)
-                s = 16 * group + k
-                if i == 0:
-                    products = rotated.tile([P, 2, BLOCK_HEADS, GROUP, D], F32)
-                    if s > LAST_BANK - 2 * GROUP:
-                        late.append(products)
-                rope_bank(products, group, c, i)
-                if s == LAST_BANK:
-                    for first in range(0, GROUP, 2):
-                        finish(nc.vector, late[0], group, c - 1, first, 2, 2)
-                    for tile in range(GROUP):
-                        finish(nc.vector, late[1], group, c, tile, 1, 1)
-                elif s > LAST_BANK - 2 * GROUP:
-                    pass
-                elif s < GROUP and i % 2 == 1:
-                    finish(nc.gpsimd, products, group, c, i - 1, 2, GROUP if i == GROUP - 1 else 0)
-                elif s >= GROUP and i == GROUP - 1:
-                    finish(nc.gpsimd, products, group, c, 0, GROUP, GROUP)
-                if s == 2 * GROUP:
+        flipped = {}
+        s = 0
+        for c, first in patches:
+            products = rotated.tile([P, 2, BLOCK_HEADS, PATCH, D], F32)
+            straight, crossed = products[:, 0], products[:, 1]
+            for i in range(PATCH):
+                rope_bank(products, c, first + i)
+                if s == 1:
+                    add_halves(nc.gpsimd, straight[:, :, 0:2], straight[:, :, 0:2], crossed[:, :, 0:2])
+                if s == 3:
+                    add_halves(nc.gpsimd, straight[:, :, 2:4], straight[:, :, 2:4], crossed[:, :, 2:4])
+                    store(nc.sync, c, first, PATCH, straight)
+                if s == 2 * PATCH:
                     nc.scalar.copy(out=tables_rest[:, 1, :, 0:HALF], in_=sin_rest[:, :, HALF:D])
                     nc.scalar.copy(out=tables_rest[:, 1, :, HALF:D], in_=sin_rest[:, :, 0:HALF])
                 for kind, n in behind[s]:
                     if kind == "flip":
-                        if n < GROUP or n % GROUP == 0:
-                            grouped = stage.tile(
-                                [P, 1 if n < GROUP else GROUP, PASSES, P, 2], F32, align_bytes=64
-                            )
-                        flip_tile(n, grouped, 0 if n < GROUP else n % GROUP)
+                        count = 1 if n < PATCH else PATCH
+                        if n % count == 0:
+                            grouped = stage.tile([P, count, PASSES, P, 2], F32, align_bytes=64)
+                            flipped[n] = grouped
+                        flip_tile(n, flipped[n - n % count], n % count)
                     if kind == "quantise":
-                        quantise_tiles(n, 1 if n < GROUP else GROUP, grouped)
+                        quantise_tiles(n, 1 if n < PATCH else PATCH, flipped[n])
                     if kind == "v":
-                        patch, i_v = divmod(n, GROUP)
-                        if i_v == 0:
-                            plain = copied.tile([P, BLOCK_HEADS, GROUP, D], F32)
-                        v_bank(plain, patch // 2, 4 + patch % 2, i_v)
+                        c_v, j_v = divmod(n, TILES)
+                        if j_v % V_PATCH == 0:
+                            plain = copied.tile([P, BLOCK_HEADS, V_PATCH, D], F32)
+                        v_bank(plain, 4 + c_v, j_v)
+                s += 1
+            if s > LAST_BANK + 1 - VECTOR_PATCHES * PATCH:
+                late.append((c, first, straight, crossed))
+            elif first > 0 and c < 2:
+                if first == PATCH:
+                    sums = summed.tile([P, BLOCK_HEADS, 2 * PATCH, D], F32)
+                some = slice(first - PATCH, first)
+                add_halves(nc.gpsimd, sums[:, :, some, :], straight, crossed)
+                if first == 2 * PATCH:
+                    store(nc.sync, c, PATCH, 2 * PATCH, sums[:])
+            elif s > PATCH:
+                add_halves(nc.gpsimd, straight, straight, crossed)
+                store(nc.sync, c, first, PATCH, straight)
+        for c, first, straight, crossed in late:
+            step = PATCH if first + PATCH < TILES else PATCH // 2
+            for i in range(0, PATCH, step):
+                some = slice(i, i + step)
+                add_halves(nc.vector, straight[:, :, some], straight[:, :, some], crossed[:, :, some])
+                store(nc.sync, c, first + i, step, straight[:, :, some])

@@ -26,11 +26,9 @@ BLOCK = BLOCK_HEADS * D
 BLOCKS = 3 * C // BLOCK
 ROPE_BLOCKS = 4
 PATCH = 4
-V_PATCH = 6
 
 WARM_UP = 5
 LAST_BANK = ROPE_BLOCKS * TILES - 1
-VECTOR_PATCHES = 2
 
 FLOPS = 2 * T * C * 3 * C
 
@@ -59,7 +57,7 @@ def tile_swaattention_pa_kernel(
         x_sb = keep.tile([P, TILES, C], BF16)
         w_q = keep.tile([P, 2, PASSES, 2 * BLOCK], U8, align_bytes=64)
         w_k = keep.tile([P, PASSES, 4 * BLOCK], U8, align_bytes=64)
-        w_v = keep.tile([P, PASSES, 4 * BLOCK], U8, align_bytes=64)
+        w_v = keep.tile([P, 2, PASSES, 2 * BLOCK], U8, align_bytes=64)
         w_planes_first = keep.tile([P, PASSES, BLOCK], U8, align_bytes=64)
         w_planes_rest = keep.tile([P, PASSES, 3 * C - BLOCK], U8, align_bytes=64)
         tables_head = keep.tile([P, 2, PATCH, D], BF16)
@@ -105,9 +103,10 @@ def tile_swaattention_pa_kernel(
         load_x(3, 1)
         load_scales(w_planes_rest, slice(BLOCK // 4, 3 * C // 4))
         load_w(w_q[:, 1], 1, 1)
-        load_w(w_v[:], 4, 2)
+        load_w(w_v[:, 0], 4, 1)
         load_x(PATCH, PATCH)
         load_w(w_k[:], 2, 2)
+        load_w(w_v[:, 1], 5, 1)
         load_tables(tables_rest, sin_rest, slice(PATCH, TILES))
         load_x(2 * PATCH, PATCH)
 
@@ -132,8 +131,12 @@ def tile_swaattention_pa_kernel(
             )
 
         def project(bank, j, c):
-            half = slice((c % 2) * 2 * BLOCK, (c % 2 + 1) * 2 * BLOCK)
-            words = w_q[:, c] if c < 2 else (w_k if c < 4 else w_v)[:, :, half]
+            kind, part = divmod(c, 2)
+            words = (
+                w_q[:, part],
+                w_k[:, :, part * 2 * BLOCK : (part + 1) * 2 * BLOCK],
+                w_v[:, part],
+            )[kind]
             for g in range(PASSES):
                 nc.tensor.matmul_mx(
                     out=bank[:],
@@ -182,11 +185,9 @@ def tile_swaattention_pa_kernel(
                 op=ALU.mult,
             )
 
-        def v_bank(plain, c, j):
+        def v_bank(plain, place, c, j):
             bank = psum_side.tile([P, BLOCK], F32)
-            nc.scalar.copy(out=plain[:, :, j % V_PATCH, :], in_=project(bank, j, c))
-            if j % V_PATCH == V_PATCH - 1:
-                store(nc.scalar, c, j - V_PATCH + 1, V_PATCH, plain[:])
+            nc.scalar.copy(out=plain[:, :, place, :], in_=project(bank, j, c))
 
         patches = [(c, 0) for c in range(ROPE_BLOCKS)]
         patches.extend((c, j) for c in range(ROPE_BLOCKS) for j in range(PATCH, TILES, PATCH))
@@ -198,11 +199,14 @@ def tile_swaattention_pa_kernel(
         behind[1].extend([("flip", 3), ("quantise", 3)])
         for n in range(PATCH):
             behind[5 + 2 * n].append(("flip", PATCH + n))
-            behind[12 + n].append(("flip", 2 * PATCH + n))
+            behind[14 + n].append(("flip", 2 * PATCH + n))
         behind[13].append(("quantise", PATCH))
         behind[17].append(("quantise", 2 * PATCH))
-        room = [6, 8, 10]
-        room.extend(range(16, LAST_BANK))
+        v_patches = [(4, 0, PATCH), (5, 0, PATCH), (4, PATCH, PATCH), (4, 2 * PATCH, PATCH)]
+        v_patches.append((5, PATCH, 2 * PATCH))
+        v_banks = [(c, first, n, i) for c, first, n in v_patches for i in range(n)]
+        room = [4, 6, 8, 10, 12, 13]
+        room.extend(range(18, LAST_BANK))
         for n in range(2 * TILES):
             behind[room[n]].append(("v", n))
 
@@ -219,13 +223,16 @@ def tile_swaattention_pa_kernel(
             quantise_tiles(j, 1, grouped)
         nc.vector.tensor_copy(out=tables_head[:, 1, :, 0:HALF], in_=sin_head[:, :, HALF:D])
         nc.vector.tensor_copy(out=tables_head[:, 1, :, HALF:D], in_=sin_head[:, :, 0:HALF])
-        late = []
         flipped = {}
         s = 0
         for c, first in patches:
             products = rotated.tile([P, 2, BLOCK_HEADS, PATCH, D], F32)
             straight, crossed = products[:, 0], products[:, 1]
             for i in range(PATCH):
+                if s == LAST_BANK:
+                    straight_2, crossed_2 = by_vector
+                    add_halves(nc.vector, straight_2, straight_2, crossed_2)
+                    store(nc.sync, *patches[-2], PATCH, straight_2)
                 rope_bank(products, c, first + i)
                 if s == 1:
                     add_halves(nc.gpsimd, straight[:, :, 0:2], straight[:, :, 0:2], crossed[:, :, 0:2])
@@ -245,13 +252,20 @@ def tile_swaattention_pa_kernel(
                     if kind == "quantise":
                         quantise_tiles(n, 1 if n < PATCH else PATCH, flipped[n])
                     if kind == "v":
-                        c_v, j_v = divmod(n, TILES)
-                        if j_v % V_PATCH == 0:
-                            plain = copied.tile([P, BLOCK_HEADS, V_PATCH, D], F32)
-                        v_bank(plain, 4 + c_v, j_v)
+                        c_v, first_v, count, place = v_banks[n]
+                        if place == 0:
+                            plain = copied.tile([P, BLOCK_HEADS, count, D], F32)
+                        v_bank(plain, place, c_v, first_v + place)
+                        if place == count - 1:
+                            store(nc.scalar, c_v, first_v, count, plain[:])
                 s += 1
-            if s > LAST_BANK + 1 - VECTOR_PATCHES * PATCH:
-                late.append((c, first, straight, crossed))
+            if (c, first) == patches[-2]:
+                by_vector = straight, crossed
+            elif (c, first) == patches[-1]:
+                for i in (0, PATCH // 2):
+                    some = slice(i, i + PATCH // 2)
+                    add_halves(nc.vector, straight[:, :, some], straight[:, :, some], crossed[:, :, some])
+                    store(nc.sync, c, first + i, PATCH // 2, straight[:, :, some])
             elif first > 0 and c < 2:
                 if first == PATCH:
                     sums = summed.tile([P, BLOCK_HEADS, 2 * PATCH, D], F32)
@@ -262,9 +276,3 @@ def tile_swaattention_pa_kernel(
             elif s > PATCH:
                 add_halves(nc.gpsimd, straight, straight, crossed)
                 store(nc.sync, c, first, PATCH, straight)
-        for c, first, straight, crossed in late:
-            step = PATCH if first + PATCH < TILES else PATCH // 2
-            for i in range(0, PATCH, step):
-                some = slice(i, i + step)
-                add_halves(nc.vector, straight[:, :, some], straight[:, :, some], crossed[:, :, some])
-                store(nc.sync, c, first + i, step, straight[:, :, some])

from contextlib import ExitStack

import concourse.mybir as mybir
from concourse.masks import make_identity

F32 = mybir.dt.float32
BF16 = mybir.dt.bfloat16
I32 = mybir.dt.int32
U32 = mybir.dt.uint32
U8 = mybir.dt.uint8
FP8X4 = mybir.dt.float8_e4m3fn_x4
FP4X4 = mybir.dt.float4_e2m1fn_x4
ALU = mybir.AluOpType

P = 128
T = 1536
C = 1024
D = 128
HALF = D // 2
K_PASS = 4 * P
PASSES = C // K_PASS
WORDS = K_PASS // 2
TILES = T // P
BLOCK_HEADS = 4
BLOCK = BLOCK_HEADS * D
BLOCKS = 3 * C // BLOCK
ROPE_BLOCKS = 4
PATCH = 4

WARM_UP = 5
LAST_BANK = ROPE_BLOCKS * TILES - 1

FLOPS = 2 * T * C * 3 * C


def tile_swaattention_pa_kernel(
    tc, x, freqs_cos, freqs_sin, w_attn_words, w_attn_scales, out_0, out_1, out_2
):
    nc = tc.nc
    outs = [out_0, out_1, out_2]

    x_rows = x[0].rearrange("(p j) c -> p j c", j=TILES)
    cos_rows = freqs_cos.rearrange("(p j) d -> p j d", j=TILES)
    sin_rows = freqs_sin.rearrange("(p j) d -> p j d", j=TILES)
    words_dram = w_attn_words.bitcast(I32).rearrange("g p n -> p g n")
    scales_dram = w_attn_scales.bitcast(I32).rearrange("g q n -> q g n")

    with ExitStack() as ctx:
        keep = ctx.enter_context(tc.tile_pool(name="keep", bufs=1))
        stage = ctx.enter_context(tc.tile_pool(name="stage", bufs=3))
        rotated = ctx.enter_context(tc.tile_pool(name="rotated", bufs=5))
        summed = ctx.enter_context(tc.tile_pool(name="summed", bufs=2))
        copied = ctx.enter_context(tc.tile_pool(name="copied", bufs=2))
        psum_rope = ctx.enter_context(tc.psum_pool(name="psum_rope", bufs=5))
        psum_side = ctx.enter_context(tc.psum_pool(name="psum_side", bufs=3))

        x_sb = keep.tile([P, TILES, C], BF16)
        w_q = keep.tile([P, 2, PASSES, 2 * BLOCK], U8, align_bytes=64)
        w_k = keep.tile([P, PASSES, 4 * BLOCK], U8, align_bytes=64)
        w_v = keep.tile([P, 2, PASSES, 2 * BLOCK], U8, align_bytes=64)
        w_planes_first = keep.tile([P, PASSES, BLOCK], U8, align_bytes=64)
        w_planes_rest = keep.tile([P, PASSES, 3 * C - BLOCK], U8, align_bytes=64)
        tables_head = keep.tile([P, 2, PATCH, D], BF16)
        tables_rest = keep.tile([P, 2, TILES - PATCH, D], BF16)
        sin_head = keep.tile([P, PATCH, D], BF16)
        sin_rest = keep.tile([P, TILES - PATCH, D], BF16)
        ident = keep.tile([P, P], F32)
        warm = keep.tile([P, BLOCK], BF16)
        x_codes = keep.tile([P, TILES, PASSES * P], U32, align_bytes=64)
        x_planes = keep.tile([P, TILES, PASSES * P], U8, align_bytes=64)

        nc.gpsimd.memset(warm[:], 0.0)
        nc.vector.memset(w_planes_first[:].bitcast(I32), 0)
        nc.vector.memset(w_planes_rest[:].bitcast(I32), 0)
        make_identity(nc, ident[:])

        def load_x(first, count):
            nc.sync.dma_start(
                out=x_sb[:, first : first + count, :], in_=x_rows[:, first : first + count, :]
            )

        def load_w(words, c, blocks):
            cols = slice(c * BLOCK // 2, (c + blocks) * BLOCK // 2)
            nc.sync.dma_start(out=words.bitcast(I32), in_=words_dram[:, :, cols])

        def load_tables(tables, sin_sb, tiles):
            nc.sync.dma_start(out=tables[:, 0], in_=cos_rows[:, tiles, :])
            nc.sync.dma_start(out=sin_sb[:], in_=sin_rows[:, tiles, :])

        def load_scales(planes, cols):
            for quadrant in range(4):
                nc.sync.dma_start(
                    out=planes[32 * quadrant : 32 * quadrant + 4].bitcast(I32),
                    in_=scales_dram[4 * quadrant : 4 * quadrant + 4, :, cols],
                )

        load_x(0, 1)
        load_x(1, 1)
        load_w(w_q[:, 0], 0, 1)
        load_scales(w_planes_first, slice(0, BLOCK // 4))
        load_tables(tables_head, sin_head, slice(0, PATCH))
        load_x(2, 1)
        load_x(3, 1)
        load_scales(w_planes_rest, slice(BLOCK // 4, 3 * C // 4))
        load_w(w_q[:, 1], 1, 1)
        load_w(w_v[:, 0], 4, 1)
        load_x(PATCH, PATCH)
        load_w(w_k[:], 2, 2)
        load_w(w_v[:, 1], 5, 1)
        load_tables(tables_rest, sin_rest, slice(PATCH, TILES))
        load_x(2 * PATCH, PATCH)

        def flip_tile(j, grouped, place):
            x_words = x_sb[:, j, :].bitcast(F32)
            bank = psum_side.tile([P, BLOCK], F32)
            words = bank[:].rearrange("p (g u m) -> p g u m", u=2, m=P)
            for g in range(PASSES):
                for u in range(2):
                    nc.tensor.transpose(
                        words[:, g, u, :],
                        x_words[:, g * WORDS + u : (g + 1) * WORDS : 2],
                        ident[:],
                    )
            nc.scalar.copy(out=grouped[:, place], in_=words.rearrange("p g u m -> p g m u"))

        def quantise_tiles(first, count, grouped):
            nc.vector.quantize_mx(
                out=x_codes[:, first : first + count, :].rearrange("p j c -> p (j c)").bitcast(FP8X4),
                scales=x_planes[:, first : first + count, :].rearrange("p j c -> p (j c)"),
                in_=grouped[:].rearrange("p j g m u -> p (j g m u)").bitcast(BF16),
            )

        def project(bank, j, c):
            kind, part = divmod(c, 2)
            words = (
                w_q[:, part],
                w_k[:, :, part * 2 * BLOCK : (part + 1) * 2 * BLOCK],
                w_v[:, part],
            )[kind]
            for g in range(PASSES):
                nc.tensor.matmul_mx(
                    out=bank[:],
                    lhsT=x_codes[:, j, g * P : (g + 1) * P].bitcast(FP8X4),
                    lhsT_scale=x_planes[:, j, g * P : (g + 1) * P],
                    rhs=words[:, g, :].bitcast(FP4X4),
                    rhs_scale=(
                        w_planes_first[:, g, :]
                        if c == 0
                        else w_planes_rest[:, g, (c - 1) * BLOCK : c * BLOCK]
                    ),
                    start=(g == 0),
                    stop=(g == PASSES - 1),
                )
            return bank[:].rearrange("p (h d) -> p h d", d=D)

        def store(queue, c, first, count, result):
            heads = slice((c % 2) * BLOCK_HEADS, (c % 2 + 1) * BLOCK_HEADS)
            rows = outs[c // 2][0, heads].rearrange("h (p j) d -> p h j d", j=TILES)
            queue.dma_start(out=rows[:, :, first : first + count, :], in_=result)

        def add_halves(engine, result, straight, crossed):
            engine.tensor_tensor(
                out=result[:, :, :, 0:HALF],
                in0=straight[:, :, :, 0:HALF],
                in1=crossed[:, :, :, HALF:D],
                op=ALU.subtract,
            )
            engine.tensor_tensor(
                out=result[:, :, :, HALF:D],
                in0=straight[:, :, :, HALF:D],
                in1=crossed[:, :, :, 0:HALF],
                op=ALU.add,
            )

        def table_of(j):
            return tables_head[:, :, j, :] if j < PATCH else tables_rest[:, :, j - PATCH, :]

        def rope_bank(products, c, j):
            rope = psum_rope.tile([P, BLOCK], F32)
            bank = project(rope, j, c)
            nc.vector.tensor_tensor(
                out=products[:, :, :, j % PATCH, :],
                in0=table_of(j).unsqueeze(2).to_broadcast([P, 2, BLOCK_HEADS, D]),
                in1=bank.unsqueeze(1).to_broadcast([P, 2, BLOCK_HEADS, D]),
                op=ALU.mult,
            )

        def v_bank(plain, place, c, j):
            bank = psum_side.tile([P, BLOCK], F32)
            nc.scalar.copy(out=plain[:, :, place, :], in_=project(bank, j, c))

        patches = [(c, 0) for c in range(ROPE_BLOCKS)]
        patches.extend((c, j) for c in range(ROPE_BLOCKS) for j in range(PATCH, TILES, PATCH))

        behind = {}
        for s in range(LAST_BANK + 1):
            behind[s] = []
        behind[0].extend([("flip", 2), ("quantise", 2)])
        behind[1].extend([("flip", 3), ("quantise", 3)])
        for n in range(PATCH):
            behind[5 + 2 * n].append(("flip", PATCH + n))
            behind[14 + n].append(("flip", 2 * PATCH + n))
        behind[13].append(("quantise", PATCH))
        behind[17].append(("quantise", 2 * PATCH))
        v_patches = [(4, 0, PATCH), (5, 0, PATCH), (4, PATCH, PATCH), (4, 2 * PATCH, PATCH)]
        v_patches.append((5, PATCH, 2 * PATCH))
        v_banks = [(c, first, n, i) for c, first, n in v_patches for i in range(n)]
        room = [4, 6, 8, 10, 12, 13]
        room.extend(range(18, LAST_BANK))
        for n in range(2 * TILES):
            behind[room[n]].append(("v", n))

        ctx.enter_context(
            tc.manual_schedule(engines={mybir.EngineType.PE, mybir.EngineType.DVE})
        )
        rope = psum_rope.tile([P, BLOCK], F32)
        for n in range(WARM_UP):
            nc.tensor.matmul(rope[:], lhsT=warm[:, 0:P], rhs=warm[:], start=True, stop=True)

        for j in range(2):
            grouped = stage.tile([P, 1, PASSES, P, 2], F32, align_bytes=64)
            flip_tile(j, grouped, 0)
            quantise_tiles(j, 1, grouped)
        nc.vector.tensor_copy(out=tables_head[:, 1, :, 0:HALF], in_=sin_head[:, :, HALF:D])
        nc.vector.tensor_copy(out=tables_head[:, 1, :, HALF:D], in_=sin_head[:, :, 0:HALF])
        flipped = {}
        s = 0
        for c, first in patches:
            products = rotated.tile([P, 2, BLOCK_HEADS, PATCH, D], F32)
            straight, crossed = products[:, 0], products[:, 1]
            for i in range(PATCH):
                if s == LAST_BANK:
                    straight_2, crossed_2 = by_vector
                    add_halves(nc.vector, straight_2, straight_2, crossed_2)
                    store(nc.sync, *patches[-2], PATCH, straight_2)
                rope_bank(products, c, first + i)
                if s == 1:
                    add_halves(nc.gpsimd, straight[:, :, 0:2], straight[:, :, 0:2], crossed[:, :, 0:2])
                if s == 3:
                    add_halves(nc.gpsimd, straight[:, :, 2:4], straight[:, :, 2:4], crossed[:, :, 2:4])
                    store(nc.sync, c, first, PATCH, straight)
                if s == 2 * PATCH:
                    nc.scalar.copy(out=tables_rest[:, 1, :, 0:HALF], in_=sin_rest[:, :, HALF:D])
                    nc.scalar.copy(out=tables_rest[:, 1, :, HALF:D], in_=sin_rest[:, :, 0:HALF])
                for kind, n in behind[s]:
                    if kind == "flip":
                        count = 1 if n < PATCH else PATCH
                        if n % count == 0:
                            grouped = stage.tile([P, count, PASSES, P, 2], F32, align_bytes=64)
                            flipped[n] = grouped
                        flip_tile(n, flipped[n - n % count], n % count)
                    if kind == "quantise":
                        quantise_tiles(n, 1 if n < PATCH else PATCH, flipped[n])
                    if kind == "v":
                        c_v, first_v, count, place = v_banks[n]
                        if place == 0:
                            plain = copied.tile([P, BLOCK_HEADS, count, D], F32)
                        v_bank(plain, place, c_v, first_v + place)
                        if place == count - 1:
                            store(nc.scalar, c_v, first_v, count, plain[:])
                s += 1
            if (c, first) == patches[-2]:
                by_vector = straight, crossed
            elif (c, first) == patches[-1]:
                for i in (0, PATCH // 2):
                    some = slice(i, i + PATCH // 2)
                    add_halves(nc.vector, straight[:, :, some], straight[:, :, some], crossed[:, :, some])
                    store(nc.sync, c, first + i, PATCH // 2, straight[:, :, some])
            elif first > 0 and c < 2:
                if first == PATCH:
                    sums = summed.tile([P, BLOCK_HEADS, 2 * PATCH, D], F32)
                some = slice(first - PATCH, first)
                add_halves(nc.gpsimd, sums[:, :, some, :], straight, crossed)
                if first == 2 * PATCH:
                    store(nc.sync, c, PATCH, 2 * PATCH, sums[:])
            elif s > PATCH:
                add_halves(nc.gpsimd, straight, straight, crossed)
                store(nc.sync, c, first, PATCH, straight)
